import numpy as np
import ml_dtypes


def mxq(x, axis, fmt="e4m3"):
    dtype, down = {"e4m3": (ml_dtypes.float8_e4m3fn, 7), "e5m2": (ml_dtypes.float8_e5m2, 14)}[fmt]
    v = np.moveaxis(np.asarray(x, np.float32).astype(ml_dtypes.bfloat16).astype(np.float64), axis, -1)
    blocks = v.reshape(v.shape[:-1] + (-1, 32))
    amax = np.abs(blocks).max(-1, keepdims=True)
    byte = np.maximum(np.where(amax > 0, np.frexp(amax)[1] - 1 + 127, 0) - down, 1)
    scale = np.exp2(byte - 127.0)
    codes = (blocks / scale).astype(np.float32).astype(dtype).astype(np.float64)
    return np.moveaxis((codes * scale).reshape(v.shape), -1, axis)


WIDE = False


def mx_kscale(k):
    if not WIDE:
        return np.ones(k)
    levels = np.array([10, -10, 5, -5, 0])
    a = np.random.permutation(np.resize(levels, k // 512 * 4)).reshape(k // 512, 4)
    idx = np.arange(k)
    return np.exp2(a[idx // 512, idx % 128 // 32])


BF16 = ml_dtypes.bfloat16


def bf(x):
    return np.asarray(x, np.float32).astype(BF16)


def f64(x):
    return np.asarray(x).astype(np.float64)


B, H, S, D = 1, 2, 2048, 256
D2 = D // 2
LAMBDA_INIT = 0.8
EPS = 1e-5


def softmax(v):
    e = np.exp(v - v.max(-1, keepdims=True))
    return e / e.sum(-1, keepdims=True)


def setup_inputs():
    s = mx_kscale(S)
    c = np.log(2.0) * np.sqrt(D2)
    q = np.random.standard_normal((B, H, S, D))
    k = np.random.standard_normal((B, H, S, D))
    q[..., 0] = c
    q[..., D2] = c
    k[..., 0] += np.log2(s)
    k[..., D2] += np.log2(s)
    v = np.random.standard_normal((B, H, S, D)) * 0.005 * np.sqrt(S) / s[:, None] * s.mean()
    return {"query": bf(q), "key": bf(k), "value": bf(v),
            "lambda_params": bf(0.3 + 0.5 * np.random.random(H))}


def reference(query, key, value, lambda_params):
    query, key, value, lambda_params = f64(query), f64(key), f64(value), f64(lambda_params)
    scale = 1.0 / np.sqrt(D2)
    q1, q2 = query[..., :D2], query[..., D2:]
    k1, k2 = key[..., :D2], key[..., D2:]
    a1 = softmax(q1 @ k1.transpose(0, 1, 3, 2) * scale)
    a2 = softmax(q2 @ k2.transpose(0, 1, 3, 2) * scale)
    lam = lambda_params[None, :, None, None]
    attn = a1 - lam * a2
    out = mxq(attn, 3, "e4m3") @ mxq(value, 2, "e4m3")
    mean = out.mean(-1, keepdims=True)
    var = ((out - mean) ** 2).mean(-1, keepdims=True)
    out = (out - mean) / np.sqrt(var + EPS)
    return out * (1.0 - LAMBDA_INIT)

@@ -1,0 +1,282 @@
+import math
+from contextlib import ExitStack
+
+import concourse.bass as bass
+import concourse.mybir as mybir
+import concourse.tile as tile
+from concourse.masks import make_identity
+
+F32 = mybir.dt.float32
+BF16 = mybir.dt.bfloat16
+U32 = mybir.dt.uint32
+U8 = mybir.dt.uint8
+FP8X4 = mybir.dt.float8_e4m3fn_x4
+ALU = mybir.AluOpType
+ACT = mybir.ActivationFunctionType
+AX = mybir.AxisListType
+
+P = 128
+H = 2
+S = 2048
+D = 256
+D2 = 128
+NT = S // P
+NB = S // 512
+SCALE = 1.0 / math.sqrt(D2)
+EPS = 1e-5
+GAIN = 0.2
+FLOPS = H * (2 * 2 * S * S * D2 + 2 * S * S * D)
+
+TCOPY = ("s", "s", "s", "v")
+
+
+def tile_differentialattention_kernel(tc, query, key, value, lambda_params, out):
+    nc = tc.nc
+    with ExitStack() as ctx:
+        const = ctx.enter_context(tc.tile_pool(name="const", bufs=1))
+        raw = ctx.enter_context(tc.tile_pool(name="raw", bufs=2))
+        keep = ctx.enter_context(tc.tile_pool(name="keep", bufs=1))
+        work = ctx.enter_context(tc.tile_pool(name="work", bufs=4))
+        grp = ctx.enter_context(tc.tile_pool(name="grp", bufs=3))
+        small = ctx.enter_context(tc.tile_pool(name="small", bufs=6))
+        outp = ctx.enter_context(tc.tile_pool(name="outp", bufs=3))
+        psc = ctx.enter_context(tc.psum_pool(name="psc", bufs=3))
+        pat = ctx.enter_context(tc.psum_pool(name="pat", bufs=3))
+        pso = ctx.enter_context(tc.psum_pool(name="pso", bufs=2))
+
+        kraw = {}
+        qraw = {}
+        vraw = {}
+        for h in range(H):
+            kr = raw.tile([P, NT, D], BF16, tag="kraw")
+            qr = raw.tile([P, NT, D], BF16, tag="qraw")
+            vr = raw.tile([P, NT, D], BF16, tag="vraw")
+            kraw[h] = kr
+            qraw[h] = qr
+            vraw[h] = vr
+            kv = key[0, h].rearrange("(n p) d -> p n d", p=P)
+            qv = query[0, h].rearrange("(n p) d -> p n d", p=P)
+            vv = value[0, h].rearrange("(n p) d -> p n d", p=P)
+            if h == 0:
+                nc.sync.dma_start(out=kr[:, 0:4, :], in_=kv[:, 0:4, :])
+                nc.sync.dma_start(out=qr[:, 0:4, :], in_=qv[:, 0:4, :])
+                for c in range(1, 4):
+                    nc.sync.dma_start(out=kr[:, 4 * c : 4 * c + 4, :], in_=kv[:, 4 * c : 4 * c + 4, :])
+                nc.sync.dma_start(out=qr[:, 4:16, :], in_=qv[:, 4:16, :])
+            else:
+                nc.sync.dma_start(out=kr[:], in_=kv)
+                nc.sync.dma_start(out=qr[:], in_=qv)
+            nc.sync.dma_start(out=vr[:], in_=vv)
+
+        ident_bf = const.tile([P, P], BF16, name="ident_bf")
+        make_identity(nc, ident_bf[:])
+        ident_f = const.tile([P, P], F32, name="ident_f")
+        make_identity(nc, ident_f[:])
+        lam_bf = const.tile([P, H], BF16, name="lam_bf")
+        nc.sync.dma_start(out=lam_bf[:], in_=lambda_params.partition_broadcast(P))
+        neglam = const.tile([P, H], F32, name="neglam")
+        nc.vector.tensor_scalar(out=neglam[:], in0=lam_bf[:], scalar1=-1.0, scalar2=None, op0=ALU.mult)
+        mhalf = const.tile([P, 1], F32, name="mhalf")
+        nc.vector.memset(mhalf[:], -0.5)
+        warm = const.tile([P, 1], F32, name="warm")
+        nc.scalar.activation(out=warm[:], in_=mhalf[:], func=ACT.Exp)
+
+        qT = {}
+        kT = {}
+        vcod = {}
+        vpl = {}
+        for h in range(H):
+            for m in range(2):
+                a = keep.tile([P, S], BF16, name="qT%d%d" % (h, m))
+                b = keep.tile([P, S], BF16, name="kT%d%d" % (h, m))
+                qT[(h, m)] = a
+                kT[(h, m)] = b
+            c = keep.tile([P, NB, D], U32, name="vcod%d" % h, align_bytes=64)
+            d = keep.tile([P, NB, D], U8, name="vpl%d" % h, align_bytes=64)
+            vcod[h] = c
+            vpl[h] = d
+
+        flip = [0]
+
+        def prep_unit(src, dst, n0, m):
+            pt = pat.tile([P, 4, P], BF16, tag="at")
+            for a in range(4):
+                nc.tensor.transpose(pt[:, a, :], src[:, n0 + a, m * P : (m + 1) * P], ident_bf[:])
+            o_ap = dst[:, n0 * P : (n0 + 4) * P]
+            i_ap = pt[:].rearrange("p a q -> p (a q)")
+            if flip[0] % 2 == 0:
+                nc.scalar.copy(out=o_ap, in_=i_ap)
+            else:
+                nc.vector.tensor_copy(out=o_ap, in_=i_ap)
+            flip[0] += 1
+
+        def prep_v(h):
+            vg = raw.tile([P, NB, D, 4], BF16, tag="vgrp", align_bytes=64)
+            for g in range(NB):
+                nc.vector.tensor_copy(out=vg[:, g], in_=vraw[h][:, 4 * g : 4 * g + 4, :].rearrange("p t d -> p d t"))
+            nc.vector.quantize_mx(
+                out=vcod[h][:].rearrange("p g d -> p (g d)").bitcast(FP8X4),
+                scales=vpl[h][:].rearrange("p g d -> p (g d)"),
+                in_=vg[:].rearrange("p g d t -> p (g d t)"),
+            )
+
+        st = {}
+
+        def stage_a(x):
+            h, i = divmod(x, NT)
+            rec = {}
+            for m in range(2):
+                sc = work.tile([P, S], F32, tag="sc%d" % m)
+                mn = small.tile([P, NB], F32, tag="mn%d" % m)
+                for j in range(NB):
+                    ps = psc.tile([P, 512], F32, tag="ps")
+                    nc.tensor.matmul(
+                        ps[:],
+                        lhsT=qT[(h, m)][:, i * P : (i + 1) * P],
+                        rhs=kT[(h, m)][:, j * 512 : (j + 1) * 512],
+                        start=True,
+                        stop=True,
+                    )
+                    nc.vector.tensor_scalar(
+                        out=sc[:, j * 512 : (j + 1) * 512],
+                        in0=ps[:],
+                        scalar1=-SCALE,
+                        scalar2=None,
+                        op0=ALU.mult,
+                        op1=ALU.min,
+                        accum_out=mn[:, j : j + 1],
+                    )
+                nm = small.tile([P, 1], F32, tag="nm%d" % m)
+                nc.vector.tensor_reduce(out=nm[:], in_=mn[:], axis=AX.X, op=ALU.min)
+                rec["sc%d" % m] = sc
+                rec["nm%d" % m] = nm
+            st[x] = rec
+
+        def stage_b(x):
+            rec = st[x]
+            sums = small.tile([P, 2], F32, tag="sums")
+            for m in range(2):
+                sc = rec["sc%d" % m]
+                nc.scalar.activation(
+                    out=sc[:], in_=sc[:], func=ACT.Exp, bias=rec["nm%d" % m][:], scale=-1.0, accum_out=sums[:, m : m + 1]
+                )
+            rr = small.tile([P, 2], F32, tag="rr")
+            nc.vector.reciprocal(out=rr[:], in_=sums[:])
+            rec["rr"] = rr
+
+        def stage_c(x):
+            h, i = divmod(x, NT)
+            rec = st[x]
+            rr = rec["rr"]
+            nc.gpsimd.tensor_scalar(
+                out=rec["sc0"][:], in0=rec["sc0"][:], scalar1=rr[:, 0:1], scalar2=0.0, op0=ALU.mult, op1=ALU.add
+            )
+            nc.gpsimd.tensor_scalar(
+                out=rec["sc1"][:],
+                in0=rec["sc1"][:],
+                scalar1=rr[:, 1:2],
+                scalar2=neglam[:, h : h + 1],
+                op0=ALU.mult,
+                op1=ALU.mult,
+            )
+
+        def stage_d(x):
+            rec = st[x]
+            gr = grp.tile([P, NB, P, 4], BF16, tag="gr", align_bytes=64)
+            for g in range(NB):
+                at = pat.tile([P, 4, P], F32, tag="at")
+                for t in range(4):
+                    c0 = (4 * g + t) * P
+                    nc.tensor.matmul(
+                        at[:, t, :], lhsT=rec["sc0"][:, c0 : c0 + P], rhs=ident_f[:], is_transpose=True, start=True, stop=False
+                    )
+                    nc.tensor.matmul(
+                        at[:, t, :], lhsT=rec["sc1"][:, c0 : c0 + P], rhs=ident_f[:], is_transpose=True, start=False, stop=True
+                    )
+                src = at[:].rearrange("p t q -> p q t")
+                if TCOPY[g] == "s":
+                    nc.scalar.copy(out=gr[:, g], in_=src)
+                else:
+                    nc.vector.tensor_copy(out=gr[:, g], in_=src)
+            rec["gr"] = gr
+
+        def stage_e(x):
+            h, i = divmod(x, NT)
+            rec = st[x]
+            cod = grp.tile([P, NB * P], U32, tag="cod", align_bytes=64)
+            pl = grp.tile([P, NB * P], U8, tag="pl", align_bytes=64)
+            nc.vector.quantize_mx(
+                out=cod[:].bitcast(FP8X4), scales=pl[:], in_=rec["gr"][:].rearrange("p g q t -> p (g q t)")
+            )
+            o = pso.tile([P, D], F32, tag="o")
+            for g in range(NB):
+                nc.tensor.matmul_mx(
+                    out=o[:],
+                    lhsT=cod[:, g * P : (g + 1) * P].bitcast(FP8X4),
+                    lhsT_scale=pl[:, g * P : (g + 1) * P],
+                    rhs=vcod[h][:, g, :].bitcast(FP8X4),
+                    rhs_scale=vpl[h][:, g, :],
+                    start=(g == 0),
+                    stop=(g == NB - 1),
+                )
+            rec["o"] = o
+
+        def stage_f(x):
+            h, i = divmod(x, NT)
+            rec = st[x]
+            o = rec["o"]
+            bs = small.tile([P, 6], F32, tag="bs")
+            nc.vector.bn_stats(out=bs[:], in_=o[:])
+            mv = small.tile([P, 2], F32, tag="mv")
+            nc.vector.bn_aggr(out=mv[:], in_=bs[:])
+            v25 = small.tile([P, 1], F32, tag="v25")
+            nc.gpsimd.tensor_scalar(
+                out=v25[:], in0=mv[:, 1:2], scalar1=1.0 / (GAIN * GAIN), scalar2=EPS / (GAIN * GAIN), op0=ALU.mult, op1=ALU.add
+            )
+            rs = small.tile([P, 1], F32, tag="rs")
+            nc.gpsimd.tensor_tensor(out=rs[:], in0=v25[:], in1=mhalf[:], op=ALU.pow)
+            nb = small.tile([P, 1], F32, tag="nb")
+            nc.gpsimd.tensor_scalar(out=nb[:], in0=mv[:, 0:1], scalar1=rs[:], scalar2=-1.0, op0=ALU.mult, op1=ALU.mult)
+            res = outp.tile([P, D], F32, tag="res")
+            nc.scalar.activation(out=res[:], in_=o[:], func=ACT.Identity, bias=nb[:], scale=rs[:])
+            nc.sync.dma_start(out=out[0, h, i * P : (i + 1) * P, :], in_=res[:])
+
+        for n0 in range(0, NT, 4):
+            for m in range(2):
+                prep_unit(kraw[0], kT[(0, m)], n0, m)
+            if n0 == 0:
+                for m in range(2):
+                    prep_unit(qraw[0], qT[(0, m)], 0, m)
+        later = []
+        for n0 in range(4, NT, 4):
+            for m in range(2):
+                later.append((qraw[0], qT[(0, m)], n0, m))
+        for n0 in range(0, NT, 4):
+            for m in range(2):
+                later.append((kraw[1], kT[(1, m)], n0, m))
+                later.append((qraw[1], qT[(1, m)], n0, m))
+
+        total = H * NT
+        pos = [0]
+        for x in range(total + 5):
+            if x < total:
+                stage_a(x)
+            if x == 1:
+                prep_v(0)
+            if x == 8:
+                prep_v(1)
+            for rep in range(2):
+                if pos[0] < len(later):
+                    u = later[pos[0]]
+                    pos[0] += 1
+                    prep_unit(u[0], u[1], u[2], u[3])
+            if 0 <= x - 1 < total:
+                stage_b(x - 1)
+            if 0 <= x - 2 < total:
+                stage_c(x - 2)
+            if 0 <= x - 3 < total:
+                stage_d(x - 3)
+            if 0 <= x - 4 < total:
+                stage_e(x - 4)
+            if 0 <= x - 5 < total:
+                stage_f(x - 5)

@@ -1,9 +1,7 @@
 import math
 from contextlib import ExitStack
 
-import concourse.bass as bass
 import concourse.mybir as mybir
-import concourse.tile as tile
 from concourse.masks import make_identity
 
 F32 = mybir.dt.float32
@@ -26,8 +24,7 @@ SCALE = 1.0 / math.sqrt(D2)
 EPS = 1e-5
 GAIN = 0.2
 FLOPS = H * (2 * 2 * S * S * D2 + 2 * S * S * D)
-
-TCOPY = ("s", "s", "s", "v")
+TOTAL = H * NT
 
 
 def tile_differentialattention_kernel(tc, query, key, value, lambda_params, out):
@@ -43,10 +40,14 @@ def tile_differentialattention_kernel(tc, query, key, value, lambda_params, out)
         psc = ctx.enter_context(tc.psum_pool(name="psc", bufs=3))
         pat = ctx.enter_context(tc.psum_pool(name="pat", bufs=3))
         pso = ctx.enter_context(tc.psum_pool(name="pso", bufs=2))
+        ctx.enter_context(tc.manual_schedule())
 
+        lam_bf = const.tile([P, H], BF16, name="lam_bf")
+        nc.sync.dma_start(out=lam_bf[:], in_=lambda_params.partition_broadcast(P))
         kraw = {}
         qraw = {}
         vraw = {}
+        views = {}
         for h in range(H):
             kr = raw.tile([P, NT, D], BF16, tag="kraw")
             qr = raw.tile([P, NT, D], BF16, tag="qraw")
@@ -54,37 +55,35 @@ def tile_differentialattention_kernel(tc, query, key, value, lambda_params, out)
             kraw[h] = kr
             qraw[h] = qr
             vraw[h] = vr
-            kv = key[0, h].rearrange("(n p) d -> p n d", p=P)
-            qv = query[0, h].rearrange("(n p) d -> p n d", p=P)
-            vv = value[0, h].rearrange("(n p) d -> p n d", p=P)
-            if h == 0:
-                nc.sync.dma_start(out=kr[:, 0:4, :], in_=kv[:, 0:4, :])
-                nc.sync.dma_start(out=qr[:, 0:4, :], in_=qv[:, 0:4, :])
-                for c in range(1, 4):
-                    nc.sync.dma_start(out=kr[:, 4 * c : 4 * c + 4, :], in_=kv[:, 4 * c : 4 * c + 4, :])
-                nc.sync.dma_start(out=qr[:, 4:16, :], in_=qv[:, 4:16, :])
-            else:
-                nc.sync.dma_start(out=kr[:], in_=kv)
-                nc.sync.dma_start(out=qr[:], in_=qv)
-            nc.sync.dma_start(out=vr[:], in_=vv)
+            views[("k", h)] = key[0, h].rearrange("(n p) d -> p n d", p=P)
+            views[("q", h)] = query[0, h].rearrange("(n p) d -> p n d", p=P)
+            views[("v", h)] = value[0, h].rearrange("(n p) d -> p n d", p=P)
+        nc.sync.dma_start(out=kraw[0][:, 0:4, :], in_=views[("k", 0)][:, 0:4, :])
+        nc.sync.dma_start(out=qraw[0][:, 0:4, :], in_=views[("q", 0)][:, 0:4, :])
+        for c in range(1, 4):
+            nc.sync.dma_start(out=kraw[0][:, 4 * c : 4 * c + 4, :], in_=views[("k", 0)][:, 4 * c : 4 * c + 4, :])
+        nc.sync.dma_start(out=vraw[0][:], in_=views[("v", 0)])
+        nc.sync.dma_start(out=qraw[0][:, 4:16, :], in_=views[("q", 0)][:, 4:16, :])
+        nc.sync.dma_start(out=kraw[1][:], in_=views[("k", 1)])
+        nc.sync.dma_start(out=qraw[1][:], in_=views[("q", 1)])
+        nc.sync.dma_start(out=vraw[1][:], in_=views[("v", 1)])
 
         ident_bf = const.tile([P, P], BF16, name="ident_bf")
         make_identity(nc, ident_bf[:])
         ident_f = const.tile([P, P], F32, name="ident_f")
         make_identity(nc, ident_f[:])
-        lam_bf = const.tile([P, H], BF16, name="lam_bf")
-        nc.sync.dma_start(out=lam_bf[:], in_=lambda_params.partition_broadcast(P))
-        neglam = const.tile([P, H], F32, name="neglam")
-        nc.vector.tensor_scalar(out=neglam[:], in0=lam_bf[:], scalar1=-1.0, scalar2=None, op0=ALU.mult)
         mhalf = const.tile([P, 1], F32, name="mhalf")
         nc.vector.memset(mhalf[:], -0.5)
         warm = const.tile([P, 1], F32, name="warm")
         nc.scalar.activation(out=warm[:], in_=mhalf[:], func=ACT.Exp)
+        neglam = const.tile([P, H], F32, name="neglam")
+        nc.vector.tensor_scalar(out=neglam[:], in0=lam_bf[:], scalar1=-1.0, scalar2=None, op0=ALU.mult)
 
         qT = {}
         kT = {}
         vcod = {}
         vpl = {}
+        vgrp = {}
         for h in range(H):
             for m in range(2):
                 a = keep.tile([P, S], BF16, name="qT%d%d" % (h, m))
@@ -93,127 +92,146 @@ def tile_differentialattention_kernel(tc, query, key, value, lambda_params, out)
                 kT[(h, m)] = b
             c = keep.tile([P, NB, D], U32, name="vcod%d" % h, align_bytes=64)
             d = keep.tile([P, NB, D], U8, name="vpl%d" % h, align_bytes=64)
+            e = keep.tile([P, NB, D, 4], BF16, name="vgrp%d" % h, align_bytes=64)
             vcod[h] = c
             vpl[h] = d
+            vgrp[h] = e
 
-        flip = [0]
-
-        def prep_unit(src, dst, n0, m):
+        def prep_unit(kind, h, n0, m):
+            src = kraw[h] if kind == "k" else qraw[h]
+            dst = kT[(h, m)] if kind == "k" else qT[(h, m)]
             pt = pat.tile([P, 4, P], BF16, tag="at")
             for a in range(4):
                 nc.tensor.transpose(pt[:, a, :], src[:, n0 + a, m * P : (m + 1) * P], ident_bf[:])
-            o_ap = dst[:, n0 * P : (n0 + 4) * P]
-            i_ap = pt[:].rearrange("p a q -> p (a q)")
-            if flip[0] % 2 == 0:
-                nc.scalar.copy(out=o_ap, in_=i_ap)
-            else:
-                nc.vector.tensor_copy(out=o_ap, in_=i_ap)
-            flip[0] += 1
+            nc.scalar.copy(out=dst[:, n0 * P : (n0 + 4) * P], in_=pt[:].rearrange("p a q -> p (a q)"))
 
-        def prep_v(h):
-            vg = raw.tile([P, NB, D, 4], BF16, tag="vgrp", align_bytes=64)
-            for g in range(NB):
-                nc.vector.tensor_copy(out=vg[:, g], in_=vraw[h][:, 4 * g : 4 * g + 4, :].rearrange("p t d -> p d t"))
+        def regroup_v(h, g):
+            nc.gpsimd.tensor_scalar(
+                out=vgrp[h][:, g],
+                in0=vraw[h][:, 4 * g : 4 * g + 4, :].rearrange("p t d -> p d t"),
+                scalar1=1.0,
+                scalar2=0.0,
+                op0=ALU.mult,
+                op1=ALU.add,
+            )
+
+        def quant_v(h):
             nc.vector.quantize_mx(
                 out=vcod[h][:].rearrange("p g d -> p (g d)").bitcast(FP8X4),
                 scales=vpl[h][:].rearrange("p g d -> p (g d)"),
-                in_=vg[:].rearrange("p g d t -> p (g d t)"),
+                in_=vgrp[h][:].rearrange("p g d t -> p (g d t)"),
             )
 
         st = {}
 
-        def stage_a(x):
+        def live(x):
+            return 0 <= x < TOTAL
+
+        def score(x, s):
             h, i = divmod(x, NT)
-            rec = {}
-            for m in range(2):
+            m, j = divmod(s, NB)
+            if s == 0:
+                st[x] = {}
+            rec = st[x]
+            if j == 0:
                 sc = work.tile([P, S], F32, tag="sc%d" % m)
                 mn = small.tile([P, NB], F32, tag="mn%d" % m)
-                for j in range(NB):
-                    ps = psc.tile([P, 512], F32, tag="ps")
-                    nc.tensor.matmul(
-                        ps[:],
-                        lhsT=qT[(h, m)][:, i * P : (i + 1) * P],
-                        rhs=kT[(h, m)][:, j * 512 : (j + 1) * 512],
-                        start=True,
-                        stop=True,
-                    )
-                    nc.vector.tensor_scalar(
-                        out=sc[:, j * 512 : (j + 1) * 512],
-                        in0=ps[:],
-                        scalar1=-SCALE,
-                        scalar2=None,
-                        op0=ALU.mult,
-                        op1=ALU.min,
-                        accum_out=mn[:, j : j + 1],
-                    )
+                rec["sc%d" % m] = sc
+                rec["mn%d" % m] = mn
+            sc = rec["sc%d" % m]
+            mn = rec["mn%d" % m]
+            ps = psc.tile([P, 512], F32, tag="ps")
+            nc.tensor.matmul(
+                ps[:],
+                lhsT=qT[(h, m)][:, i * P : (i + 1) * P],
+                rhs=kT[(h, m)][:, j * 512 : (j + 1) * 512],
+                start=True,
+                stop=True,
+            )
+            nc.vector.tensor_scalar(
+                out=sc[:, j * 512 : (j + 1) * 512],
+                in0=ps[:],
+                scalar1=-SCALE,
+                scalar2=None,
+                op0=ALU.mult,
+                op1=ALU.min,
+                accum_out=mn[:, j : j + 1],
+            )
+            if j == NB - 1:
                 nm = small.tile([P, 1], F32, tag="nm%d" % m)
                 nc.vector.tensor_reduce(out=nm[:], in_=mn[:], axis=AX.X, op=ALU.min)
-                rec["sc%d" % m] = sc
                 rec["nm%d" % m] = nm
-            st[x] = rec
 
-        def stage_b(x):
+        def expo(x, m):
             rec = st[x]
-            sums = small.tile([P, 2], F32, tag="sums")
-            for m in range(2):
-                sc = rec["sc%d" % m]
-                nc.scalar.activation(
-                    out=sc[:], in_=sc[:], func=ACT.Exp, bias=rec["nm%d" % m][:], scale=-1.0, accum_out=sums[:, m : m + 1]
+            sc = rec["sc%d" % m]
+            sm = small.tile([P, 1], F32, tag="sm%d" % m)
+            nc.scalar.activation(out=sc[:], in_=sc[:], func=ACT.Exp, bias=rec["nm%d" % m][:], scale=-1.0, accum_out=sm[:])
+            rec["sm%d" % m] = sm
+
+        def recip(x, m):
+            rec = st[x]
+            rr = small.tile([P, 1], F32, tag="rr%d" % m)
+            nc.vector.reciprocal(out=rr[:], in_=rec["sm%d" % m][:])
+            rec["rr%d" % m] = rr
+
+        def norm_map(x, m):
+            h, i = divmod(x, NT)
+            rec = st[x]
+            sc = rec["sc%d" % m]
+            if m == 0:
+                nc.gpsimd.tensor_scalar(out=sc[:], in0=sc[:], scalar1=rec["rr0"][:], scalar2=0.0, op0=ALU.mult, op1=ALU.add)
+            else:
+                nc.gpsimd.tensor_scalar(
+                    out=sc[:], in0=sc[:], scalar1=rec["rr1"][:], scalar2=neglam[:, h : h + 1], op0=ALU.mult, op1=ALU.mult
                 )
-            rr = small.tile([P, 2], F32, tag="rr")
-            nc.vector.reciprocal(out=rr[:], in_=sums[:])
-            rec["rr"] = rr
 
-        def stage_c(x):
-            h, i = divmod(x, NT)
+        def turn(x, s):
             rec = st[x]
-            rr = rec["rr"]
-            nc.gpsimd.tensor_scalar(
-                out=rec["sc0"][:], in0=rec["sc0"][:], scalar1=rr[:, 0:1], scalar2=0.0, op0=ALU.mult, op1=ALU.add
-            )
-            nc.gpsimd.tensor_scalar(
-                out=rec["sc1"][:],
-                in0=rec["sc1"][:],
-                scalar1=rr[:, 1:2],
-                scalar2=neglam[:, h : h + 1],
-                op0=ALU.mult,
-                op1=ALU.mult,
-            )
-
-        def stage_d(x):
-            rec = st[x]
-            gr = grp.tile([P, NB, P, 4], BF16, tag="gr", align_bytes=64)
-            for g in range(NB):
+            g, half = divmod(s, 2)
+            if s == 0:
+                gr = grp.tile([P, NB, P, 4], BF16, tag="gr", align_bytes=64)
+                rec["gr"] = gr
+            if half == 0:
                 at = pat.tile([P, 4, P], F32, tag="at")
-                for t in range(4):
-                    c0 = (4 * g + t) * P
-                    nc.tensor.matmul(
-                        at[:, t, :], lhsT=rec["sc0"][:, c0 : c0 + P], rhs=ident_f[:], is_transpose=True, start=True, stop=False
-                    )
-                    nc.tensor.matmul(
-                        at[:, t, :], lhsT=rec["sc1"][:, c0 : c0 + P], rhs=ident_f[:], is_transpose=True, start=False, stop=True
-                    )
-                src = at[:].rearrange("p t q -> p q t")
-                if TCOPY[g] == "s":
-                    nc.scalar.copy(out=gr[:, g], in_=src)
-                else:
-                    nc.vector.tensor_copy(out=gr[:, g], in_=src)
-            rec["gr"] = gr
+                rec["at%d" % g] = at
+            at = rec["at%d" % g]
+            for t in (2 * half, 2 * half + 1):
+                c0 = (4 * g + t) * P
+                nc.tensor.matmul(
+                    at[:, t, :], lhsT=rec["sc0"][:, c0 : c0 + P], rhs=ident_f[:], is_transpose=True, start=True, stop=False
+                )
+                nc.tensor.matmul(
+                    at[:, t, :], lhsT=rec["sc1"][:, c0 : c0 + P], rhs=ident_f[:], is_transpose=True, start=False, stop=True
+                )
 
-        def stage_e(x):
-            h, i = divmod(x, NT)
+        def copy_group(x, g, eng):
+            rec = st[x]
+            src = rec["at%d" % g][:].rearrange("p t q -> p q t")
+            if eng == "s":
+                nc.scalar.copy(out=rec["gr"][:, g], in_=src)
+            else:
+                nc.vector.tensor_copy(out=rec["gr"][:, g], in_=src)
+
+        def quant(x):
             rec = st[x]
             cod = grp.tile([P, NB * P], U32, tag="cod", align_bytes=64)
             pl = grp.tile([P, NB * P], U8, tag="pl", align_bytes=64)
             nc.vector.quantize_mx(
                 out=cod[:].bitcast(FP8X4), scales=pl[:], in_=rec["gr"][:].rearrange("p g q t -> p (g q t)")
             )
+            rec["cod"] = cod
+            rec["pl"] = pl
+
+        def pv(x):
+            h, i = divmod(x, NT)
+            rec = st[x]
             o = pso.tile([P, D], F32, tag="o")
             for g in range(NB):
                 nc.tensor.matmul_mx(
                     out=o[:],
-                    lhsT=cod[:, g * P : (g + 1) * P].bitcast(FP8X4),
-                    lhsT_scale=pl[:, g * P : (g + 1) * P],
+                    lhsT=rec["cod"][:, g * P : (g + 1) * P].bitcast(FP8X4),
+                    lhsT_scale=rec["pl"][:, g * P : (g + 1) * P],
                     rhs=vcod[h][:, g, :].bitcast(FP8X4),
                     rhs_scale=vpl[h][:, g, :],
                     start=(g == 0),
@@ -221,12 +239,10 @@ def tile_differentialattention_kernel(tc, query, key, value, lambda_params, out)
                 )
             rec["o"] = o
 
-        def stage_f(x):
-            h, i = divmod(x, NT)
+        def stats(x):
             rec = st[x]
-            o = rec["o"]
             bs = small.tile([P, 6], F32, tag="bs")
-            nc.vector.bn_stats(out=bs[:], in_=o[:])
+            nc.vector.bn_stats(out=bs[:], in_=rec["o"][:])
             mv = small.tile([P, 2], F32, tag="mv")
             nc.vector.bn_aggr(out=mv[:], in_=bs[:])
             v25 = small.tile([P, 1], F32, tag="v25")
@@ -237,46 +253,76 @@ def tile_differentialattention_kernel(tc, query, key, value, lambda_params, out)
             nc.gpsimd.tensor_tensor(out=rs[:], in0=v25[:], in1=mhalf[:], op=ALU.pow)
             nb = small.tile([P, 1], F32, tag="nb")
             nc.gpsimd.tensor_scalar(out=nb[:], in0=mv[:, 0:1], scalar1=rs[:], scalar2=-1.0, op0=ALU.mult, op1=ALU.mult)
+            rec["rs"] = rs
+            rec["nb"] = nb
+
+        def finish(x):
+            h, i = divmod(x, NT)
+            rec = st[x]
             res = outp.tile([P, D], F32, tag="res")
-            nc.scalar.activation(out=res[:], in_=o[:], func=ACT.Identity, bias=nb[:], scale=rs[:])
+            nc.scalar.activation(out=res[:], in_=rec["o"][:], func=ACT.Identity, bias=rec["nb"][:], scale=rec["rs"][:])
             nc.sync.dma_start(out=out[0, h, i * P : (i + 1) * P, :], in_=res[:])
 
-        for n0 in range(0, NT, 4):
-            for m in range(2):
-                prep_unit(kraw[0], kT[(0, m)], n0, m)
-            if n0 == 0:
-                for m in range(2):
-                    prep_unit(qraw[0], qT[(0, m)], 0, m)
         later = []
-        for n0 in range(4, NT, 4):
+        for n0 in (4, 8, 12):
             for m in range(2):
-                later.append((qraw[0], qT[(0, m)], n0, m))
-        for n0 in range(0, NT, 4):
+                later.append(("q", 0, n0, m))
+        for n0 in (0, 4, 8, 12):
             for m in range(2):
-                later.append((kraw[1], kT[(1, m)], n0, m))
-                later.append((qraw[1], qT[(1, m)], n0, m))
-
-        total = H * NT
+                later.append(("k", 1, n0, m))
+        for n0 in (0, 4, 8, 12):
+            for m in range(2):
+                later.append(("q", 1, n0, m))
         pos = [0]
-        for x in range(total + 5):
-            if x < total:
-                stage_a(x)
+
+        def next_unit():
+            if pos[0] < len(later):
+                u = later[pos[0]]
+                pos[0] += 1
+                prep_unit(u[0], u[1], u[2], u[3])
+
+        for g in range(NB):
+            regroup_v(0, g)
+
+        for x in range(TOTAL + 5):
+            if live(x - 1):
+                norm_map(x - 1, 0)
+                expo(x - 1, 1)
+            for s in range(8):
+                if x == 0:
+                    m, j = divmod(s, NB)
+                    prep_unit("k", 0, 4 * j, m)
+                    if j == 0:
+                        prep_unit("q", 0, 0, m)
+                if live(x):
+                    score(x, s)
+                if live(x - 2):
+                    turn(x - 2, s)
+                    if s in (1, 3, 5):
+                        copy_group(x - 2, s // 2, "s")
+                if s == 1 and live(x - 4):
+                    finish(x - 4)
+                if s == 3 and live(x):
+                    expo(x, 0)
+                if s == 2 and live(x - 3):
+                    pv(x - 3)
+                if s == 4 and live(x - 3):
+                    stats(x - 3)
+                if s == 3 and live(x - 1):
+                    recip(x - 1, 1)
+                    norm_map(x - 1, 1)
+            if 1 <= x:
+                next_unit()
+                if x <= 3:
+                    next_unit()
+            if 3 <= x <= 6:
+                regroup_v(1, x - 3)
+            if live(x - 2):
+                copy_group(x - 2, 3, "v")
+                quant(x - 2)
             if x == 1:
-                prep_v(0)
+                quant_v(0)
             if x == 8:
-                prep_v(1)
-            for rep in range(2):
-                if pos[0] < len(later):
-                    u = later[pos[0]]
-                    pos[0] += 1
-                    prep_unit(u[0], u[1], u[2], u[3])
-            if 0 <= x - 1 < total:
-                stage_b(x - 1)
-            if 0 <= x - 2 < total:
-                stage_c(x - 2)
-            if 0 <= x - 3 < total:
-                stage_d(x - 3)
-            if 0 <= x - 4 < total:
-                stage_e(x - 4)
-            if 0 <= x - 5 < total:
-                stage_f(x - 5)
+                quant_v(1)
+            if live(x):
+                recip(x, 0)

@@ -318,7 +318,7 @@ def tile_differentialattention_kernel(tc, query, key, value, lambda_params, out)
             if 3 <= x <= 6:
                 regroup_v(1, x - 3)
             if live(x - 2):
-                copy_group(x - 2, 3, "v")
+                copy_group(x - 2, 3, "s")
                 quant(x - 2)
             if x == 1:
                 quant_v(0)

@@ -25,6 +25,7 @@ EPS = 1e-5
 GAIN = 0.2
 FLOPS = H * (2 * 2 * S * S * D2 + 2 * S * S * D)
 TOTAL = H * NT
+VCUT = 1536
 
 
 def tile_differentialattention_kernel(tc, query, key, value, lambda_params, out):
@@ -180,11 +181,28 @@ def tile_differentialattention_kernel(tc, query, key, value, lambda_params, out)
             rec = st[x]
             sc = rec["sc%d" % m]
             if m == 0:
-                nc.gpsimd.tensor_scalar(out=sc[:], in0=sc[:], scalar1=rec["rr0"][:], scalar2=0.0, op0=ALU.mult, op1=ALU.add)
+                nc.gpsimd.tensor_scalar(
+                    out=sc[:, 0:VCUT], in0=sc[:, 0:VCUT], scalar1=rec["rr0"][:], scalar2=0.0, op0=ALU.mult, op1=ALU.add
+                )
             else:
                 nc.gpsimd.tensor_scalar(
                     out=sc[:], in0=sc[:], scalar1=rec["rr1"][:], scalar2=neglam[:, h : h + 1], op0=ALU.mult, op1=ALU.mult
                 )
+
+        def add_on_vector(x):
+            rec = st[x]
+            ab = grp.tile([P, S - VCUT], BF16, tag="ab")
+            nc.vector.scalar_tensor_tensor(
+                out=ab[:], in0=rec["sc0"][:, VCUT:S], scalar=rec["rr0"][:], in1=rec["sc1"][:, VCUT:S], op0=ALU.mult, op1=ALU.add
+            )
+            rec["ab"] = ab
+
+        def turn_bf(x):
+            rec = st[x]
+            at = pat.tile([P, 4, P], BF16, tag="at")
+            rec["at3"] = at
+            for t in range(4):
+                nc.tensor.transpose(at[:, t, :], rec["ab"][:, t * P : (t + 1) * P], ident_bf[:])
 
         def turn(x, s):
             rec = st[x]
@@ -297,7 +315,11 @@ def tile_differentialattention_kernel(tc, query, key, value, lambda_params, out)
                 if live(x):
                     score(x, s)
                 if live(x - 2):
-                    turn(x - 2, s)
+                    if s < 6:
+                        turn(x - 2, s)
+                    if s == 6:
+                        turn_bf(x - 2)
+                        copy_group(x - 2, 3, "s")
                     if s in (1, 3, 5):
                         copy_group(x - 2, s // 2, "s")
                 if s == 1 and live(x - 4):
@@ -318,8 +340,9 @@ def tile_differentialattention_kernel(tc, query, key, value, lambda_params, out)
             if 3 <= x <= 6:
                 regroup_v(1, x - 3)
             if live(x - 2):
-                copy_group(x - 2, 3, "s")
                 quant(x - 2)
+            if live(x - 1):
+                add_on_vector(x - 1)
             if x == 1:
                 quant_v(0)
             if x == 8:

@@ -25,7 +25,16 @@ EPS = 1e-5
 GAIN = 0.2
 FLOPS = H * (2 * 2 * S * S * D2 + 2 * S * S * D)
 TOTAL = H * NT
-VCUT = 1536
+FIRST = (
+    (("k", 0, 0), ("q", 0, 0), ("k", 4, 0)),
+    (("k", 8, 0),),
+    (("k", 12, 0),),
+    (("k", 0, 1), ("q", 0, 1)),
+    (("k", 4, 1),),
+    (("k", 8, 1),),
+    (("k", 12, 1),),
+    (),
+)
 
 
 def tile_differentialattention_kernel(tc, query, key, value, lambda_params, out):
@@ -180,29 +189,13 @@ def tile_differentialattention_kernel(tc, query, key, value, lambda_params, out)
             h, i = divmod(x, NT)
             rec = st[x]
             sc = rec["sc%d" % m]
+            eng = nc.vector if x == TOTAL - 1 else nc.gpsimd
             if m == 0:
-                nc.gpsimd.tensor_scalar(
-                    out=sc[:, 0:VCUT], in0=sc[:, 0:VCUT], scalar1=rec["rr0"][:], scalar2=0.0, op0=ALU.mult, op1=ALU.add
-                )
+                eng.tensor_scalar(out=sc[:], in0=sc[:], scalar1=rec["rr0"][:], scalar2=0.0, op0=ALU.mult, op1=ALU.add)
             else:
-                nc.gpsimd.tensor_scalar(
+                eng.tensor_scalar(
                     out=sc[:], in0=sc[:], scalar1=rec["rr1"][:], scalar2=neglam[:, h : h + 1], op0=ALU.mult, op1=ALU.mult
                 )
-
-        def add_on_vector(x):
-            rec = st[x]
-            ab = grp.tile([P, S - VCUT], BF16, tag="ab")
-            nc.vector.scalar_tensor_tensor(
-                out=ab[:], in0=rec["sc0"][:, VCUT:S], scalar=rec["rr0"][:], in1=rec["sc1"][:, VCUT:S], op0=ALU.mult, op1=ALU.add
-            )
-            rec["ab"] = ab
-
-        def turn_bf(x):
-            rec = st[x]
-            at = pat.tile([P, 4, P], BF16, tag="at")
-            rec["at3"] = at
-            for t in range(4):
-                nc.tensor.transpose(at[:, t, :], rec["ab"][:, t * P : (t + 1) * P], ident_bf[:])
 
         def turn(x, s):
             rec = st[x]
@@ -308,23 +301,17 @@ def tile_differentialattention_kernel(tc, query, key, value, lambda_params, out)
                 expo(x - 1, 1)
             for s in range(8):
                 if x == 0:
-                    m, j = divmod(s, NB)
-                    prep_unit("k", 0, 4 * j, m)
-                    if j == 0:
-                        prep_unit("q", 0, 0, m)
+                    for u in FIRST[s]:
+                        prep_unit(u[0], 0, u[1], u[2])
                 if live(x):
                     score(x, s)
                 if live(x - 2):
-                    if s < 6:
-                        turn(x - 2, s)
-                    if s == 6:
-                        turn_bf(x - 2)
-                        copy_group(x - 2, 3, "s")
+                    turn(x - 2, s)
                     if s in (1, 3, 5):
                         copy_group(x - 2, s // 2, "s")
                 if s == 1 and live(x - 4):
                     finish(x - 4)
-                if s == 3 and live(x):
+                if s == (3 if x > 0 else 7) and live(x):
                     expo(x, 0)
                 if s == 2 and live(x - 3):
                     pv(x - 3)
@@ -340,9 +327,8 @@ def tile_differentialattention_kernel(tc, query, key, value, lambda_params, out)
             if 3 <= x <= 6:
                 regroup_v(1, x - 3)
             if live(x - 2):
+                copy_group(x - 2, 3, "s")
                 quant(x - 2)
-            if live(x - 1):
-                add_on_vector(x - 1)
             if x == 1:
                 quant_v(0)
             if x == 8:

@@ -44,7 +44,7 @@ def tile_differentialattention_kernel(tc, query, key, value, lambda_params, out)
         raw = ctx.enter_context(tc.tile_pool(name="raw", bufs=2))
         keep = ctx.enter_context(tc.tile_pool(name="keep", bufs=1))
         work = ctx.enter_context(tc.tile_pool(name="work", bufs=4))
-        grp = ctx.enter_context(tc.tile_pool(name="grp", bufs=3))
+        grp = ctx.enter_context(tc.tile_pool(name="grp", bufs=4))
         small = ctx.enter_context(tc.tile_pool(name="small", bufs=6))
         outp = ctx.enter_context(tc.tile_pool(name="outp", bufs=3))
         psc = ctx.enter_context(tc.psum_pool(name="psc", bufs=3))
@@ -256,6 +256,11 @@ def tile_differentialattention_kernel(tc, query, key, value, lambda_params, out)
             nc.vector.bn_stats(out=bs[:], in_=rec["o"][:])
             mv = small.tile([P, 2], F32, tag="mv")
             nc.vector.bn_aggr(out=mv[:], in_=bs[:])
+            rec["mv"] = mv
+
+        def stats_g(x):
+            rec = st[x]
+            mv = rec["mv"]
             v25 = small.tile([P, 1], F32, tag="v25")
             nc.gpsimd.tensor_scalar(
                 out=v25[:], in0=mv[:, 1:2], scalar1=1.0 / (GAIN * GAIN), scalar2=EPS / (GAIN * GAIN), op0=ALU.mult, op1=ALU.add
@@ -295,9 +300,12 @@ def tile_differentialattention_kernel(tc, query, key, value, lambda_params, out)
         for g in range(NB):
             regroup_v(0, g)
 
-        for x in range(TOTAL + 5):
+        for x in range(TOTAL + 6):
             if live(x - 1):
                 norm_map(x - 1, 0)
+            if live(x - 5):
+                stats_g(x - 5)
+            if live(x - 1):
                 expo(x - 1, 1)
             for s in range(8):
                 if x == 0:
@@ -309,14 +317,14 @@ def tile_differentialattention_kernel(tc, query, key, value, lambda_params, out)
                     turn(x - 2, s)
                     if s in (1, 3, 5):
                         copy_group(x - 2, s // 2, "s")
-                if s == 1 and live(x - 4):
-                    finish(x - 4)
                 if s == (3 if x > 0 else 7) and live(x):
                     expo(x, 0)
-                if s == 2 and live(x - 3):
-                    pv(x - 3)
-                if s == 4 and live(x - 3):
-                    stats(x - 3)
+                if s == 3 and live(x - 5):
+                    finish(x - 5)
+                if s == 2 and live(x - 4):
+                    pv(x - 4)
+                if s == 4 and live(x - 4):
+                    stats(x - 4)
                 if s == 3 and live(x - 1):
                     recip(x - 1, 1)
                     norm_map(x - 1, 1)
@@ -328,7 +336,8 @@ def tile_differentialattention_kernel(tc, query, key, value, lambda_params, out)
                 regroup_v(1, x - 3)
             if live(x - 2):
                 copy_group(x - 2, 3, "s")
-                quant(x - 2)
+            if live(x - 3):
+                quant(x - 3)
             if x == 1:
                 quant_v(0)
             if x == 8:

import math
from contextlib import ExitStack

import concourse.mybir as mybir
from concourse.masks import make_identity

F32 = mybir.dt.float32
BF16 = mybir.dt.bfloat16
U32 = mybir.dt.uint32
U8 = mybir.dt.uint8
FP8X4 = mybir.dt.float8_e4m3fn_x4
ALU = mybir.AluOpType
ACT = mybir.ActivationFunctionType
AX = mybir.AxisListType

P = 128
H = 2
S = 2048
D = 256
D2 = 128
NT = S // P
NB = S // 512
SCALE = 1.0 / math.sqrt(D2)
EPS = 1e-5
GAIN = 0.2
FLOPS = H * (2 * 2 * S * S * D2 + 2 * S * S * D)
TOTAL = H * NT
FIRST = (
    (("k", 0, 0), ("q", 0, 0), ("k", 4, 0)),
    (("k", 8, 0),),
    (("k", 12, 0),),
    (("k", 0, 1), ("q", 0, 1)),
    (("k", 4, 1),),
    (("k", 8, 1),),
    (("k", 12, 1),),
    (),
)


def tile_differentialattention_kernel(tc, query, key, value, lambda_params, out):
    nc = tc.nc
    with ExitStack() as ctx:
        const = ctx.enter_context(tc.tile_pool(name="const", bufs=1))
        raw = ctx.enter_context(tc.tile_pool(name="raw", bufs=2))
        keep = ctx.enter_context(tc.tile_pool(name="keep", bufs=1))
        work = ctx.enter_context(tc.tile_pool(name="work", bufs=4))
        grp = ctx.enter_context(tc.tile_pool(name="grp", bufs=4))
        small = ctx.enter_context(tc.tile_pool(name="small", bufs=6))
        outp = ctx.enter_context(tc.tile_pool(name="outp", bufs=3))
        psc = ctx.enter_context(tc.psum_pool(name="psc", bufs=3))
        pat = ctx.enter_context(tc.psum_pool(name="pat", bufs=3))
        pso = ctx.enter_context(tc.psum_pool(name="pso", bufs=2))
        ctx.enter_context(tc.manual_schedule())

        lam_bf = const.tile([P, H], BF16, name="lam_bf")
        nc.sync.dma_start(out=lam_bf[:], in_=lambda_params.partition_broadcast(P))
        kraw = {}
        qraw = {}
        vraw = {}
        views = {}
        for h in range(H):
            kr = raw.tile([P, NT, D], BF16, tag="kraw")
            qr = raw.tile([P, NT, D], BF16, tag="qraw")
            vr = raw.tile([P, NT, D], BF16, tag="vraw")
            kraw[h] = kr
            qraw[h] = qr
            vraw[h] = vr
            views[("k", h)] = key[0, h].rearrange("(n p) d -> p n d", p=P)
            views[("q", h)] = query[0, h].rearrange("(n p) d -> p n d", p=P)
            views[("v", h)] = value[0, h].rearrange("(n p) d -> p n d", p=P)
        nc.sync.dma_start(out=kraw[0][:, 0:4, :], in_=views[("k", 0)][:, 0:4, :])
        nc.sync.dma_start(out=qraw[0][:, 0:4, :], in_=views[("q", 0)][:, 0:4, :])
        for c in range(1, 4):
            nc.sync.dma_start(out=kraw[0][:, 4 * c : 4 * c + 4, :], in_=views[("k", 0)][:, 4 * c : 4 * c + 4, :])
        nc.sync.dma_start(out=vraw[0][:], in_=views[("v", 0)])
        nc.sync.dma_start(out=qraw[0][:, 4:16, :], in_=views[("q", 0)][:, 4:16, :])
        nc.sync.dma_start(out=kraw[1][:], in_=views[("k", 1)])
        nc.sync.dma_start(out=qraw[1][:], in_=views[("q", 1)])
        nc.sync.dma_start(out=vraw[1][:], in_=views[("v", 1)])

        ident_bf = const.tile([P, P], BF16, name="ident_bf")
        make_identity(nc, ident_bf[:])
        ident_f = const.tile([P, P], F32, name="ident_f")
        make_identity(nc, ident_f[:])
        mhalf = const.tile([P, 1], F32, name="mhalf")
        nc.vector.memset(mhalf[:], -0.5)
        warm = const.tile([P, 1], F32, name="warm")
        nc.scalar.activation(out=warm[:], in_=mhalf[:], func=ACT.Exp)
        neglam = const.tile([P, H], F32, name="neglam")
        nc.vector.tensor_scalar(out=neglam[:], in0=lam_bf[:], scalar1=-1.0, scalar2=None, op0=ALU.mult)

        qT = {}
        kT = {}
        vcod = {}
        vpl = {}
        vgrp = {}
        for h in range(H):
            for m in range(2):
                a = keep.tile([P, S], BF16, name="qT%d%d" % (h, m))
                b = keep.tile([P, S], BF16, name="kT%d%d" % (h, m))
                qT[(h, m)] = a
                kT[(h, m)] = b
            c = keep.tile([P, NB, D], U32, name="vcod%d" % h, align_bytes=64)
            d = keep.tile([P, NB, D], U8, name="vpl%d" % h, align_bytes=64)
            e = keep.tile([P, NB, D, 4], BF16, name="vgrp%d" % h, align_bytes=64)
            vcod[h] = c
            vpl[h] = d
            vgrp[h] = e

        def prep_unit(kind, h, n0, m):
            src = kraw[h] if kind == "k" else qraw[h]
            dst = kT[(h, m)] if kind == "k" else qT[(h, m)]
            pt = pat.tile([P, 4, P], BF16, tag="at")
            for a in range(4):
                nc.tensor.transpose(pt[:, a, :], src[:, n0 + a, m * P : (m + 1) * P], ident_bf[:])
            nc.scalar.copy(out=dst[:, n0 * P : (n0 + 4) * P], in_=pt[:].rearrange("p a q -> p (a q)"))

        def regroup_v(h, g):
            nc.gpsimd.tensor_scalar(
                out=vgrp[h][:, g],
                in0=vraw[h][:, 4 * g : 4 * g + 4, :].rearrange("p t d -> p d t"),
                scalar1=1.0,
                scalar2=0.0,
                op0=ALU.mult,
                op1=ALU.add,
            )

        def quant_v(h):
            nc.vector.quantize_mx(
                out=vcod[h][:].rearrange("p g d -> p (g d)").bitcast(FP8X4),
                scales=vpl[h][:].rearrange("p g d -> p (g d)"),
                in_=vgrp[h][:].rearrange("p g d t -> p (g d t)"),
            )

        st = {}

        def live(x):
            return 0 <= x < TOTAL

        def score(x, s):
            h, i = divmod(x, NT)
            m, j = divmod(s, NB)
            if s == 0:
                st[x] = {}
            rec = st[x]
            if j == 0:
                sc = work.tile([P, S], F32, tag="sc%d" % m)
                mn = small.tile([P, NB], F32, tag="mn%d" % m)
                rec["sc%d" % m] = sc
                rec["mn%d" % m] = mn
            sc = rec["sc%d" % m]
            mn = rec["mn%d" % m]
            ps = psc.tile([P, 512], F32, tag="ps")
            nc.tensor.matmul(
                ps[:],
                lhsT=qT[(h, m)][:, i * P : (i + 1) * P],
                rhs=kT[(h, m)][:, j * 512 : (j + 1) * 512],
                start=True,
                stop=True,
            )
            nc.vector.tensor_scalar(
                out=sc[:, j * 512 : (j + 1) * 512],
                in0=ps[:],
                scalar1=-SCALE,
                scalar2=None,
                op0=ALU.mult,
                op1=ALU.min,
                accum_out=mn[:, j : j + 1],
            )
            if j == NB - 1:
                nm = small.tile([P, 1], F32, tag="nm%d" % m)
                nc.vector.tensor_reduce(out=nm[:], in_=mn[:], axis=AX.X, op=ALU.min)
                rec["nm%d" % m] = nm

        def expo(x, m):
            rec = st[x]
            sc = rec["sc%d" % m]
            sm = small.tile([P, 1], F32, tag="sm%d" % m)
            nc.scalar.activation(out=sc[:], in_=sc[:], func=ACT.Exp, bias=rec["nm%d" % m][:], scale=-1.0, accum_out=sm[:])
            rec["sm%d" % m] = sm

        def recip(x, m):
            rec = st[x]
            rr = small.tile([P, 1], F32, tag="rr%d" % m)
            nc.vector.reciprocal(out=rr[:], in_=rec["sm%d" % m][:])
            rec["rr%d" % m] = rr

        def norm_map(x, m):
            h, i = divmod(x, NT)
            rec = st[x]
            sc = rec["sc%d" % m]
            eng = nc.vector if x == TOTAL - 1 else nc.gpsimd
            if m == 0:
                eng.tensor_scalar(out=sc[:], in0=sc[:], scalar1=rec["rr0"][:], scalar2=0.0, op0=ALU.mult, op1=ALU.add)
            else:
                eng.tensor_scalar(
                    out=sc[:], in0=sc[:], scalar1=rec["rr1"][:], scalar2=neglam[:, h : h + 1], op0=ALU.mult, op1=ALU.mult
                )

        def turn(x, s):
            rec = st[x]
            g, half = divmod(s, 2)
            if s == 0:
                gr = grp.tile([P, NB, P, 4], BF16, tag="gr", align_bytes=64)
                rec["gr"] = gr
            if half == 0:
                at = pat.tile([P, 4, P], F32, tag="at")
                rec["at%d" % g] = at
            at = rec["at%d" % g]
            for t in (2 * half, 2 * half + 1):
                c0 = (4 * g + t) * P
                nc.tensor.matmul(
                    at[:, t, :], lhsT=rec["sc0"][:, c0 : c0 + P], rhs=ident_f[:], is_transpose=True, start=True, stop=False
                )
                nc.tensor.matmul(
                    at[:, t, :], lhsT=rec["sc1"][:, c0 : c0 + P], rhs=ident_f[:], is_transpose=True, start=False, stop=True
                )

        def copy_group(x, g, eng):
            rec = st[x]
            src = rec["at%d" % g][:].rearrange("p t q -> p q t")
            if eng == "s":
                nc.scalar.copy(out=rec["gr"][:, g], in_=src)
            else:
                nc.vector.tensor_copy(out=rec["gr"][:, g], in_=src)

        def quant(x):
            rec = st[x]
            cod = grp.tile([P, NB * P], U32, tag="cod", align_bytes=64)
            pl = grp.tile([P, NB * P], U8, tag="pl", align_bytes=64)
            nc.vector.quantize_mx(
                out=cod[:].bitcast(FP8X4), scales=pl[:], in_=rec["gr"][:].rearrange("p g q t -> p (g q t)")
            )
            rec["cod"] = cod
            rec["pl"] = pl

        def pv(x):
            h, i = divmod(x, NT)
            rec = st[x]
            o = pso.tile([P, D], F32, tag="o")
            for g in range(NB):
                nc.tensor.matmul_mx(
                    out=o[:],
                    lhsT=rec["cod"][:, g * P : (g + 1) * P].bitcast(FP8X4),
                    lhsT_scale=rec["pl"][:, g * P : (g + 1) * P],
                    rhs=vcod[h][:, g, :].bitcast(FP8X4),
                    rhs_scale=vpl[h][:, g, :],
                    start=(g == 0),
                    stop=(g == NB - 1),
                )
            rec["o"] = o

        def stats(x):
            rec = st[x]
            bs = small.tile([P, 6], F32, tag="bs")
            nc.vector.bn_stats(out=bs[:], in_=rec["o"][:])
            mv = small.tile([P, 2], F32, tag="mv")
            nc.vector.bn_aggr(out=mv[:], in_=bs[:])
            rec["mv"] = mv

        def stats_g(x):
            rec = st[x]
            mv = rec["mv"]
            v25 = small.tile([P, 1], F32, tag="v25")
            nc.gpsimd.tensor_scalar(
                out=v25[:], in0=mv[:, 1:2], scalar1=1.0 / (GAIN * GAIN), scalar2=EPS / (GAIN * GAIN), op0=ALU.mult, op1=ALU.add
            )
            rs = small.tile([P, 1], F32, tag="rs")
            nc.gpsimd.tensor_tensor(out=rs[:], in0=v25[:], in1=mhalf[:], op=ALU.pow)
            nb = small.tile([P, 1], F32, tag="nb")
            nc.gpsimd.tensor_scalar(out=nb[:], in0=mv[:, 0:1], scalar1=rs[:], scalar2=-1.0, op0=ALU.mult, op1=ALU.mult)
            rec["rs"] = rs
            rec["nb"] = nb

        def finish(x):
            h, i = divmod(x, NT)
            rec = st[x]
            res = outp.tile([P, D], F32, tag="res")
            nc.scalar.activation(out=res[:], in_=rec["o"][:], func=ACT.Identity, bias=rec["nb"][:], scale=rec["rs"][:])
            nc.sync.dma_start(out=out[0, h, i * P : (i + 1) * P, :], in_=res[:])

        later = []
        for n0 in (4, 8, 12):
            for m in range(2):
                later.append(("q", 0, n0, m))
        for n0 in (0, 4, 8, 12):
            for m in range(2):
                later.append(("k", 1, n0, m))
        for n0 in (0, 4, 8, 12):
            for m in range(2):
                later.append(("q", 1, n0, m))
        pos = [0]

        def next_unit():
            if pos[0] < len(later):
                u = later[pos[0]]
                pos[0] += 1
                prep_unit(u[0], u[1], u[2], u[3])

        for g in range(NB):
            regroup_v(0, g)

        for x in range(TOTAL + 6):
            if live(x - 1):
                norm_map(x - 1, 0)
            if live(x - 5):
                stats_g(x - 5)
            if live(x - 1):
                expo(x - 1, 1)
            for s in range(8):
                if x == 0:
                    for u in FIRST[s]:
                        prep_unit(u[0], 0, u[1], u[2])
                if live(x):
                    score(x, s)
                if live(x - 2):
                    turn(x - 2, s)
                    if s in (1, 3, 5):
                        copy_group(x - 2, s // 2, "s")
                if s == (3 if x > 0 else 7) and live(x):
                    expo(x, 0)
                if s == 3 and live(x - 5):
                    finish(x - 5)
                if s == 2 and live(x - 4):
                    pv(x - 4)
                if s == 4 and live(x - 4):
                    stats(x - 4)
                if s == 3 and live(x - 1):
                    recip(x - 1, 1)
                    norm_map(x - 1, 1)
            if 1 <= x:
                next_unit()
                if x <= 3:
                    next_unit()
            if 3 <= x <= 6:
                regroup_v(1, x - 3)
            if live(x - 2):
                copy_group(x - 2, 3, "s")
            if live(x - 3):
                quant(x - 3)
            if x == 1:
                quant_v(0)
            if x == 8:
                quant_v(1)
            if live(x):
                recip(x, 0)
